import numpy as np
import ml_dtypes

BF16 = ml_dtypes.bfloat16


def bf(x):
    return np.asarray(x, np.float32).astype(BF16)


def f32(x):
    return np.asarray(x, np.float32)


def f64(x):
    return np.asarray(x).astype(np.float64)


def striped(idx):
    return np.tile(idx.reshape(-1, 16).T, (8, 1))


CI, CO, S, N, G, P = 256, 256, 4096, 2048, 16, 128


def setup_inputs():
    bound = np.sqrt(6.0 / (CI + CO))
    return {"base": f32(np.random.standard_normal((CO, S))), "x": bf(np.random.standard_normal((CI, N))), "w": bf(np.random.uniform(-bound, bound, (G, CI, CO))), "bg": f32(0.1 * np.random.standard_normal((CO, G))), "offs": striped(np.random.permutation(S)[:N])}


def reference(base, x, w, bg, offs):
    idx = offs[:16].T.reshape(-1)
    xg = f64(x).reshape(CI, G, P)
    y = np.einsum('gkm,kgp->mgp', f64(w), xg) + f64(bg)[:, :, None]
    out = f64(base).copy()
    out[:, idx] = y.reshape(CO, N)
    return out

@@ -1,0 +1,71 @@
+import concourse.mybir as mybir
+
+CI, CO, S, N, G = 256, 256, 4096, 2048, 16
+P = 128
+K_ROWS = CI // P
+M_BLOCKS = CO // P
+BANK = 512
+GROUPS_PER_BANK = BANK // P
+BANKS = N // BANK
+
+FLOPS = 2 * CI * CO * N
+
+BF16, F32, U16 = mybir.dt.bfloat16, mybir.dt.float32, mybir.dt.uint16
+ADD = mybir.AluOpType.add
+COPY = mybir.ActivationFunctionType.Copy
+
+
+def tile_groupwiselinearprojector_kernel(tc, base, x, w, bg, offs, out):
+    nc = tc.nc
+    with (
+        tc.tile_pool(name="held", bufs=1) as held,
+        tc.psum_pool(name="psum", bufs=M_BLOCKS * BANKS) as psum,
+    ):
+        offsets = held.tile([P, N // 16], U16, name="offsets")
+        nc.sync.dma_start(offsets[:], offs)
+
+        bias = held.tile([P, M_BLOCKS, G], F32, name="bias")
+        nc.sync.dma_start(bias[:], bg.rearrange("(b p) g -> p b g", p=P))
+
+        x_sb = held.tile([P, K_ROWS, N], BF16, name="x_sb")
+        nc.sync.dma_start(x_sb[:], x.rearrange("(p i) j -> p i j", i=K_ROWS))
+
+        w_sb = []
+        for bank in range(BANKS):
+            w_bank = held.tile([P, GROUPS_PER_BANK, K_ROWS, CO], BF16, name=f"w_bank{bank}")
+            groups = w[bank * GROUPS_PER_BANK : (bank + 1) * GROUPS_PER_BANK]
+            nc.sync.dma_start(w_bank[:], groups.rearrange("g (p i) m -> p g i m", i=K_ROWS))
+            w_sb.append(w_bank)
+
+        windows = []
+        for b in range(M_BLOCKS):
+            window = held.tile([P, S], F32, name=f"window{b}")
+            nc.sync.dma_start(window[:], base[b * P : (b + 1) * P, :])
+            windows.append(window)
+
+        for b in range(M_BLOCKS):
+            bias_wide = held.tile([P, G, P], F32, name=f"bias_wide{b}")
+            nc.gpsimd.tensor_copy(bias_wide[:], bias[:, b, :].unsqueeze(2).to_broadcast([P, G, P]))
+
+            projected = held.tile([P, N], F32, name=f"projected{b}")
+            for bank in range(BANKS):
+                acc = psum.tile([P, BANK], F32, name="acc")
+                for q in range(GROUPS_PER_BANK):
+                    g = bank * GROUPS_PER_BANK + q
+                    for i in range(K_ROWS):
+                        nc.tensor.matmul(
+                            acc[:, q * P : (q + 1) * P],
+                            w_sb[bank][:, q, i, b * P : (b + 1) * P],
+                            x_sb[:, i, g * P : (g + 1) * P],
+                            start=(i == 0),
+                            stop=(i == K_ROWS - 1),
+                        )
+                nc.scalar.activation(projected[:, bank * BANK : (bank + 1) * BANK], acc[:], COPY)
+
+            nc.vector.tensor_tensor(
+                windows[b][:].indirect(offsets[:]),
+                projected[:],
+                bias_wide[:].rearrange("p g c -> p (g c)"),
+                ADD,
+            )
+            nc.sync.dma_start(out[b * P : (b + 1) * P, :], windows[b][:])

@@ -28,17 +28,13 @@ def tile_groupwiselinearprojector_kernel(tc, base, x, w, bg, offs, out):
         nc.sync.dma_start(bias[:], bg.rearrange("(b p) g -> p b g", p=P))
 
         x_sb = held.tile([P, K_ROWS, N], BF16, name="x_sb")
-        nc.sync.dma_start(x_sb[:], x.rearrange("(p i) j -> p i j", i=K_ROWS))
+        nc.sync.dma_start(x_sb[:], x.rearrange("(i p) j -> p i j", p=P))
 
-        w_sb = []
-        for bank in range(BANKS):
-            w_bank = held.tile([P, GROUPS_PER_BANK, K_ROWS, CO], BF16, name=f"w_bank{bank}")
-            groups = w[bank * GROUPS_PER_BANK : (bank + 1) * GROUPS_PER_BANK]
-            nc.sync.dma_start(w_bank[:], groups.rearrange("g (p i) m -> p g i m", i=K_ROWS))
-            w_sb.append(w_bank)
-
-        windows = []
+        w_sb, windows = [], []
         for b in range(M_BLOCKS):
+            w_block = held.tile([P, G, K_ROWS, P], BF16, name=f"w_block{b}")
+            nc.sync.dma_start(w_block[:], w[:, :, b * P : (b + 1) * P].rearrange("g (i p) m -> p g i m", p=P))
+            w_sb.append(w_block)
             window = held.tile([P, S], F32, name=f"window{b}")
             nc.sync.dma_start(window[:], base[b * P : (b + 1) * P, :])
             windows.append(window)
@@ -55,7 +51,7 @@ def tile_groupwiselinearprojector_kernel(tc, base, x, w, bg, offs, out):
                     for i in range(K_ROWS):
                         nc.tensor.matmul(
                             acc[:, q * P : (q + 1) * P],
-                            w_sb[bank][:, q, i, b * P : (b + 1) * P],
+                            w_sb[b][:, g, i, :],
                             x_sb[:, i, g * P : (g + 1) * P],
                             start=(i == 0),
                             stop=(i == K_ROWS - 1),

@@ -32,8 +32,12 @@ def tile_groupwiselinearprojector_kernel(tc, base, x, w, bg, offs, out):
 
         w_sb, windows = [], []
         for b in range(M_BLOCKS):
-            w_block = held.tile([P, G, K_ROWS, P], BF16, name=f"w_block{b}")
-            nc.sync.dma_start(w_block[:], w[:, :, b * P : (b + 1) * P].rearrange("g (i p) m -> p g i m", p=P))
+            w_block = []
+            for bank in range(BANKS):
+                w_bank = held.tile([P, GROUPS_PER_BANK, K_ROWS, P], BF16, name=f"w_block{b}_bank{bank}")
+                part = w[bank * GROUPS_PER_BANK : (bank + 1) * GROUPS_PER_BANK, :, b * P : (b + 1) * P]
+                nc.sync.dma_start(w_bank[:], part.rearrange("g (i p) m -> p g i m", p=P))
+                w_block.append(w_bank)
             w_sb.append(w_block)
             window = held.tile([P, S], F32, name=f"window{b}")
             nc.sync.dma_start(window[:], base[b * P : (b + 1) * P, :])
@@ -51,7 +55,7 @@ def tile_groupwiselinearprojector_kernel(tc, base, x, w, bg, offs, out):
                     for i in range(K_ROWS):
                         nc.tensor.matmul(
                             acc[:, q * P : (q + 1) * P],
-                            w_sb[b][:, g, i, :],
+                            w_sb[b][bank][:, q, i, :],
                             x_sb[:, i, g * P : (g + 1) * P],
                             start=(i == 0),
                             stop=(i == K_ROWS - 1),

@@ -60,7 +60,10 @@ def tile_groupwiselinearprojector_kernel(tc, base, x, w, bg, offs, out):
                             start=(i == 0),
                             stop=(i == K_ROWS - 1),
                         )
-                nc.scalar.activation(projected[:, bank * BANK : (bank + 1) * BANK], acc[:], COPY)
+                if b == 0:
+                    nc.vector.tensor_copy(projected[:, bank * BANK : (bank + 1) * BANK], acc[:])
+                else:
+                    nc.scalar.activation(projected[:, bank * BANK : (bank + 1) * BANK], acc[:], COPY)
 
             nc.vector.tensor_tensor(
                 windows[b][:].indirect(offsets[:]),

@@ -21,14 +21,14 @@ def tile_groupwiselinearprojector_kernel(tc, base, x, w, bg, offs, out):
         tc.tile_pool(name="held", bufs=1) as held,
         tc.psum_pool(name="psum", bufs=M_BLOCKS * BANKS) as psum,
     ):
-        offsets = held.tile([P, N // 16], U16, name="offsets")
-        nc.sync.dma_start(offsets[:], offs)
-
         bias = held.tile([P, M_BLOCKS, G], F32, name="bias")
-        nc.sync.dma_start(bias[:], bg.rearrange("(b p) g -> p b g", p=P))
+        nc.scalar.dma_start(bias[:], bg.rearrange("(b p) g -> p b g", p=P))
 
         x_sb = held.tile([P, K_ROWS, N], BF16, name="x_sb")
         nc.sync.dma_start(x_sb[:], x.rearrange("(i p) j -> p i j", p=P))
+
+        offsets = held.tile([P, N // 16], U16, name="offsets")
+        nc.sync.dma_start(offsets[:], offs)
 
         w_sb, windows = [], []
         for b in range(M_BLOCKS):

@@ -43,10 +43,13 @@ def tile_groupwiselinearprojector_kernel(tc, base, x, w, bg, offs, out):
             nc.sync.dma_start(window[:], base[b * P : (b + 1) * P, :])
             windows.append(window)
 
+        bias_wides = []
         for b in range(M_BLOCKS):
             bias_wide = held.tile([P, G, P], F32, name=f"bias_wide{b}")
-            nc.gpsimd.tensor_copy(bias_wide[:], bias[:, b, :].unsqueeze(2).to_broadcast([P, G, P]))
+            nc.vector.tensor_copy(bias_wide[:], bias[:, b, :].unsqueeze(2).to_broadcast([P, G, P]))
+            bias_wides.append(bias_wide)
 
+        for b in range(M_BLOCKS):
             projected = held.tile([P, N], F32, name=f"projected{b}")
             for bank in range(BANKS):
                 acc = psum.tile([P, BANK], F32, name="acc")
@@ -68,7 +71,7 @@ def tile_groupwiselinearprojector_kernel(tc, base, x, w, bg, offs, out):
             nc.vector.tensor_tensor(
                 windows[b][:].indirect(offsets[:]),
                 projected[:],
-                bias_wide[:].rearrange("p g c -> p (g c)"),
+                bias_wides[b][:].rearrange("p g c -> p (g c)"),
                 ADD,
             )
             nc.sync.dma_start(out[b * P : (b + 1) * P, :], windows[b][:])

@@ -30,18 +30,22 @@ def tile_groupwiselinearprojector_kernel(tc, base, x, w, bg, offs, out):
         offsets = held.tile([P, N // 16], U16, name="offsets")
         nc.sync.dma_start(offsets[:], offs)
 
-        w_sb, windows = [], []
-        for b in range(M_BLOCKS):
-            w_block = []
+        w_sb = [[] for b in range(M_BLOCKS)]
+        windows = []
+
+        def load_weights(b):
             for bank in range(BANKS):
                 w_bank = held.tile([P, GROUPS_PER_BANK, K_ROWS, P], BF16, name=f"w_block{b}_bank{bank}")
                 part = w[bank * GROUPS_PER_BANK : (bank + 1) * GROUPS_PER_BANK, :, b * P : (b + 1) * P]
                 nc.sync.dma_start(w_bank[:], part.rearrange("g (i p) m -> p g i m", p=P))
-                w_block.append(w_bank)
-            w_sb.append(w_block)
+                w_sb[b].append(w_bank)
+
+        load_weights(0)
+        for b in range(M_BLOCKS):
             window = held.tile([P, S], F32, name=f"window{b}")
             nc.sync.dma_start(window[:], base[b * P : (b + 1) * P, :])
             windows.append(window)
+        load_weights(1)
 
         bias_wides = []
         for b in range(M_BLOCKS):

@@ -6,6 +6,8 @@ K_ROWS = CI // P
 M_BLOCKS = CO // P
 BANK = 512
 GROUPS_PER_BANK = BANK // P
+W_HALVES = 2
+GROUPS_PER_HALF = G // W_HALVES
 BANKS = N // BANK
 
 FLOPS = 2 * CI * CO * N
@@ -25,7 +27,7 @@ def tile_groupwiselinearprojector_kernel(tc, base, x, w, bg, offs, out):
         nc.scalar.dma_start(bias[:], bg.rearrange("(b p) g -> p b g", p=P))
 
         x_sb = held.tile([P, K_ROWS, N], BF16, name="x_sb")
-        nc.sync.dma_start(x_sb[:], x.rearrange("(i p) j -> p i j", p=P))
+        nc.sync.dma_start(x_sb[:], x.rearrange("(p i) j -> p i j", i=K_ROWS))
 
         offsets = held.tile([P, N // 16], U16, name="offsets")
         nc.sync.dma_start(offsets[:], offs)
@@ -34,11 +36,12 @@ def tile_groupwiselinearprojector_kernel(tc, base, x, w, bg, offs, out):
         windows = []
 
         def load_weights(b):
-            for bank in range(BANKS):
-                w_bank = held.tile([P, GROUPS_PER_BANK, K_ROWS, P], BF16, name=f"w_block{b}_bank{bank}")
-                part = w[bank * GROUPS_PER_BANK : (bank + 1) * GROUPS_PER_BANK, :, b * P : (b + 1) * P]
-                nc.sync.dma_start(w_bank[:], part.rearrange("g (i p) m -> p g i m", p=P))
-                w_sb[b].append(w_bank)
+            for half in range(W_HALVES):
+                w_half = held.tile([P, K_ROWS, GROUPS_PER_HALF, P], BF16, name=f"w_block{b}_half{half}")
+                part = w[half * GROUPS_PER_HALF : (half + 1) * GROUPS_PER_HALF, :, b * P : (b + 1) * P]
+                for i in range(K_ROWS):
+                    nc.sync.dma_start(w_half[:, i, :, :], part.rearrange("g (p i) m -> i p g m", i=K_ROWS)[i])
+                w_sb[b].append(w_half)
 
         load_weights(0)
         for b in range(M_BLOCKS):
@@ -62,7 +65,7 @@ def tile_groupwiselinearprojector_kernel(tc, base, x, w, bg, offs, out):
                     for i in range(K_ROWS):
                         nc.tensor.matmul(
                             acc[:, q * P : (q + 1) * P],
-                            w_sb[b][bank][:, q, i, :],
+                            w_sb[b][g // GROUPS_PER_HALF][:, i, g % GROUPS_PER_HALF, :],
                             x_sb[:, i, g * P : (g + 1) * P],
                             start=(i == 0),
                             stop=(i == K_ROWS - 1),

@@ -81,4 +81,5 @@ def tile_groupwiselinearprojector_kernel(tc, base, x, w, bg, offs, out):
                 bias_wides[b][:].rearrange("p g c -> p (g c)"),
                 ADD,
             )
-            nc.sync.dma_start(out[b * P : (b + 1) * P, :], windows[b][:])
+            store_queue = nc.sync if b == 0 else nc.scalar
+            store_queue.dma_start(out[b * P : (b + 1) * P, :], windows[b][:])

import concourse.mybir as mybir

CI, CO, S, N, G = 256, 256, 4096, 2048, 16
P = 128
K_ROWS = CI // P
M_BLOCKS = CO // P
BANK = 512
GROUPS_PER_BANK = BANK // P
W_HALVES = 2
GROUPS_PER_HALF = G // W_HALVES
BANKS = N // BANK

FLOPS = 2 * CI * CO * N

BF16, F32, U16 = mybir.dt.bfloat16, mybir.dt.float32, mybir.dt.uint16
ADD = mybir.AluOpType.add
COPY = mybir.ActivationFunctionType.Copy


def tile_groupwiselinearprojector_kernel(tc, base, x, w, bg, offs, out):
    nc = tc.nc
    with (
        tc.tile_pool(name="held", bufs=1) as held,
        tc.psum_pool(name="psum", bufs=M_BLOCKS * BANKS) as psum,
    ):
        bias = held.tile([P, M_BLOCKS, G], F32, name="bias")
        nc.scalar.dma_start(bias[:], bg.rearrange("(b p) g -> p b g", p=P))

        x_sb = held.tile([P, K_ROWS, N], BF16, name="x_sb")
        nc.sync.dma_start(x_sb[:], x.rearrange("(p i) j -> p i j", i=K_ROWS))

        offsets = held.tile([P, N // 16], U16, name="offsets")
        nc.sync.dma_start(offsets[:], offs)

        w_sb = [[] for b in range(M_BLOCKS)]
        windows = []

        def load_weights(b):
            for half in range(W_HALVES):
                w_half = held.tile([P, K_ROWS, GROUPS_PER_HALF, P], BF16, name=f"w_block{b}_half{half}")
                part = w[half * GROUPS_PER_HALF : (half + 1) * GROUPS_PER_HALF, :, b * P : (b + 1) * P]
                for i in range(K_ROWS):
                    nc.sync.dma_start(w_half[:, i, :, :], part.rearrange("g (p i) m -> i p g m", i=K_ROWS)[i])
                w_sb[b].append(w_half)

        load_weights(0)
        for b in range(M_BLOCKS):
            window = held.tile([P, S], F32, name=f"window{b}")
            nc.sync.dma_start(window[:], base[b * P : (b + 1) * P, :])
            windows.append(window)
        load_weights(1)

        bias_wides = []
        for b in range(M_BLOCKS):
            bias_wide = held.tile([P, G, P], F32, name=f"bias_wide{b}")
            nc.vector.tensor_copy(bias_wide[:], bias[:, b, :].unsqueeze(2).to_broadcast([P, G, P]))
            bias_wides.append(bias_wide)

        for b in range(M_BLOCKS):
            projected = held.tile([P, N], F32, name=f"projected{b}")
            for bank in range(BANKS):
                acc = psum.tile([P, BANK], F32, name="acc")
                for q in range(GROUPS_PER_BANK):
                    g = bank * GROUPS_PER_BANK + q
                    for i in range(K_ROWS):
                        nc.tensor.matmul(
                            acc[:, q * P : (q + 1) * P],
                            w_sb[b][g // GROUPS_PER_HALF][:, i, g % GROUPS_PER_HALF, :],
                            x_sb[:, i, g * P : (g + 1) * P],
                            start=(i == 0),
                            stop=(i == K_ROWS - 1),
                        )
                if b == 0:
                    nc.vector.tensor_copy(projected[:, bank * BANK : (bank + 1) * BANK], acc[:])
                else:
                    nc.scalar.activation(projected[:, bank * BANK : (bank + 1) * BANK], acc[:], COPY)

            nc.vector.tensor_tensor(
                windows[b][:].indirect(offsets[:]),
                projected[:],
                bias_wides[b][:].rearrange("p g c -> p (g c)"),
                ADD,
            )
            store_queue = nc.sync if b == 0 else nc.scalar
            store_queue.dma_start(out[b * P : (b + 1) * P, :], windows[b][:])
